import numpy as np
import ml_dtypes


def mxq(x, axis, fmt="e4m3"):
    dtype, down = {"e4m3": (ml_dtypes.float8_e4m3fn, 7), "e5m2": (ml_dtypes.float8_e5m2, 14)}[fmt]
    v = np.moveaxis(np.asarray(x, np.float32).astype(ml_dtypes.bfloat16).astype(np.float64), axis, -1)
    blocks = v.reshape(v.shape[:-1] + (-1, 32))
    amax = np.abs(blocks).max(-1, keepdims=True)
    byte = np.maximum(np.where(amax > 0, np.frexp(amax)[1] - 1 + 127, 0) - down, 1)
    scale = np.exp2(byte - 127.0)
    codes = (blocks / scale).astype(np.float32).astype(dtype).astype(np.float64)
    return np.moveaxis((codes * scale).reshape(v.shape), -1, axis)


WIDE = False


def mx_kscale(k):
    if not WIDE:
        return np.ones(k)
    levels = np.array([10, -10, 5, -5, 0])
    a = np.random.permutation(np.resize(levels, k // 512 * 4)).reshape(k // 512, 4)
    idx = np.arange(k)
    return np.exp2(a[idx // 512, idx % 128 // 32])


BF16 = ml_dtypes.bfloat16


def bf(x):
    return np.asarray(x, np.float32).astype(BF16)


def f64(x):
    return np.asarray(x).astype(np.float64)


B, N, D, HID, HEADS = 2, 32, 3, 16384, 128


def silu(v):
    e = np.exp(-np.abs(v))
    return v * np.where(v >= 0, 1.0, e) / (1.0 + e)


def pairwise_dist(c):
    diff = c[:, :, None, :] - c[:, None, :, :]
    sq = np.sum(diff * diff, axis=-1)
    safe = np.where(sq > 0, sq, 1.0)
    return np.where(sq > 0, np.sqrt(safe), 0.0)


def setup_inputs():
    t = np.maximum(mx_kscale(HID), 1.0) ** 2
    return {"coords": bf(np.random.standard_normal((B, N, D))),
            "w1": bf(np.random.uniform(-1.0, 1.0, (1, HID)) * t[None, :]),
            "b1": bf(np.random.uniform(-1.0, 1.0, HID) * t),
            "w2": bf(np.random.standard_normal((HID, HEADS)) / np.sqrt(HID) / t[:, None]),
            "b2": bf(np.random.standard_normal(HEADS) * 0.3)}


def reference(coords, w1, b1, w2, b2):
    d = pairwise_dist(f64(coords))
    h = silu(d[..., None] * f64(w1)[0] + f64(b1))
    b = (mxq(h, 3, "e4m3") @ mxq(f64(w2), 0, "e4m3")) + f64(b2)
    return np.transpose(b, (0, 3, 1, 2))

@@ -1,0 +1,230 @@
+from contextlib import ExitStack
+
+import concourse.mybir as mybir
+from concourse.masks import make_identity
+
+F32 = mybir.dt.float32
+BF16 = mybir.dt.bfloat16
+U32 = mybir.dt.uint32
+U8 = mybir.dt.uint8
+FP8X4 = mybir.dt.float8_e4m3fn_x4
+ACT = mybir.ActivationFunctionType
+ALU = mybir.AluOpType
+AXIS = mybir.AxisListType
+
+BATCH = 2
+POINTS = 32
+DIM = 3
+HIDDEN = 16384
+HEADS = 128
+
+P = 128
+PACK = 4
+K_PASS = P * PACK
+PASSES = HIDDEN // K_PASS
+COLS = 512
+PAIRS = POINTS * (POINTS - 1) // 2
+USED = PAIRS + 1
+PART_COLS = COLS // P
+CHUNK = 4
+RUN = 4
+PLANE_BUFS = 3
+OUT_ROW = POINTS + 1
+
+FLOPS = 2 * BATCH * POINTS * POINTS * HIDDEN * HEADS
+
+
+def block_levels():
+    levels = []
+    offset = 0
+    m = POINTS // 2
+    while m >= 1:
+        levels.append((m, offset))
+        offset += (POINTS // (2 * m)) * m * m
+        m //= 2
+    assert offset == PAIRS
+    return levels
+
+
+def regroup(nc, grouped, planes):
+    nc.vector.tensor_copy(
+        out=grouped.rearrange("p (c i) t -> p c t i", i=RUN),
+        in_=planes.rearrange("p t (c i) -> p c t i", i=RUN),
+    )
+
+
+def tile_distancerelativebias_k_kernel(tc, coords, w1, b1, w2, b2, out):
+    nc = tc.nc
+    levels = block_levels()
+    with ExitStack() as ctx:
+        ctx.enter_context(tc.manual_schedule())
+        keep = ctx.enter_context(tc.tile_pool(name="keep", bufs=1))
+        w2_stage = ctx.enter_context(tc.tile_pool(name="w2_stage", bufs=2))
+        h_stage = ctx.enter_context(tc.tile_pool(name="h_stage", bufs=4))
+        psum = ctx.enter_context(tc.psum_pool(name="psum", bufs=1))
+
+        points = keep.tile([P, BATCH, DIM], BF16)
+        nc.vector.memset(points[:], 0.0)
+        nc.sync.dma_start(out=points[0:POINTS, :, :], in_=coords.rearrange("b i c -> i b c"))
+        rows = keep.tile([P, K_PASS], BF16)
+        nc.vector.memset(rows[2 * PASSES : P, :], 0.0)
+        nc.sync.dma_start(out=rows[0:PASSES, :], in_=w1.rearrange("o (g x) -> (o g) x", x=K_PASS))
+        nc.sync.dma_start(out=rows[PASSES : 2 * PASSES, :], in_=b1.rearrange("(g x) -> g x", x=K_PASS))
+        nc.sync.dma_start(out=rows[2 * PASSES : 2 * PASSES + 1, 0:HEADS], in_=b2.rearrange("(o k) -> o k", o=1))
+        w2_raw = keep.tile([P, PASSES, PACK * HEADS], BF16)
+        for first in range(0, PASSES, CHUNK):
+            nc.sync.dma_start(
+                out=w2_raw[:, first : first + CHUNK, :],
+                in_=w2[first * K_PASS : (first + CHUNK) * K_PASS, :].rearrange("(g p t) k -> p g (t k)", p=P, t=PACK),
+            )
+
+        ident_bf = keep.tile([P, P], BF16)
+        make_identity(nc, ident_bf[:])
+        ident_f32 = keep.tile([P, P], F32)
+        make_identity(nc, ident_f32[:])
+        one = keep.tile([P, 1], F32)
+        nc.vector.memset(one[:], 1.0)
+        warm_sqrt = keep.tile([P, 1], F32)
+        nc.scalar.activation(out=warm_sqrt[:], in_=one[:], func=ACT.Sqrt)
+
+        planes = [keep.tile([P, PACK, BATCH, COLS], BF16, name="planes%d" % r) for r in range(PLANE_BUFS)]
+        for r in range(PLANE_BUFS):
+            nc.gpsimd.memset(planes[r][:, :, :, PAIRS:COLS], 0.0)
+
+        pair_diff = keep.tile([P, COLS], BF16)
+        nc.vector.memset(pair_diff[:, PAIRS:COLS], 0.0)
+        for m, offset in levels:
+            halves = ident_bf[:, 0:POINTS].rearrange("i (q two m) -> i q two m", two=2, m=m)
+            blocks = POINTS // (2 * m)
+            nc.vector.tensor_sub(
+                out=pair_diff[:, offset : offset + blocks * m * m].rearrange("i (q a c) -> i q a c", a=m, c=m),
+                in0=halves[:, :, 0, :].unsqueeze(3).to_broadcast([P, blocks, m, m]),
+                in1=halves[:, :, 1, :].unsqueeze(2).to_broadcast([P, blocks, m, m]),
+            )
+
+        diff = psum.tile([P, PART_COLS, BATCH * DIM], F32)
+        for l in range(PART_COLS):
+            nc.tensor.matmul(
+                out=diff[:, l, :],
+                lhsT=pair_diff[:, l * P : (l + 1) * P],
+                rhs=points[:].rearrange("i b c -> i (b c)"),
+                start=True,
+                stop=True,
+            )
+        squares = keep.tile([P, PART_COLS, BATCH * DIM], F32)
+        nc.scalar.activation(out=squares[:], in_=diff[:], func=ACT.Square)
+        sq_dist = keep.tile([P, PART_COLS, BATCH], F32)
+        nc.vector.tensor_reduce(
+            out=sq_dist[:], in_=squares[:].rearrange("p l (b c) -> p l b c", c=DIM), axis=AXIS.X, op=ALU.add
+        )
+        dist_col = keep.tile([P, PART_COLS, BATCH], F32)
+        nc.scalar.activation(out=dist_col[:], in_=sq_dist[:], func=ACT.Sqrt)
+        warm_silu = keep.tile([P, 1], F32)
+        nc.scalar.activation(out=warm_silu[:], in_=dist_col[:, 0, 0:1], func=ACT.Silu)
+
+        turned = psum.tile([P, PACK + 1, P], BF16)
+        for t in range(PACK):
+            nc.tensor.transpose(turned[:, t, :], rows[:].rearrange("r (p t) -> r t p", t=PACK)[:, t, :], ident_bf[:])
+        nc.tensor.transpose(turned[:, PACK, :], rows[:, 0:P], ident_bf[:])
+        affine = keep.tile([P, PACK, 2 * PASSES], F32)
+        nc.vector.tensor_copy(out=affine[:], in_=turned[:, 0:PACK, 0 : 2 * PASSES])
+        b2_col = keep.tile([P, 1], F32)
+        nc.vector.tensor_copy(out=b2_col[:], in_=turned[:, PACK, 2 * PASSES : 2 * PASSES + 1])
+
+        dist = keep.tile([P, BATCH, COLS], F32)
+        for b in range(BATCH):
+            spread = psum.tile([P, COLS], F32, name="spread%d" % b)
+            for l in range(PART_COLS):
+                nc.tensor.transpose(
+                    spread[:, l * P : (l + 1) * P], dist_col[:, l, b : b + 1].to_broadcast([P, P]), ident_f32[:]
+                )
+            nc.vector.tensor_copy(out=dist[:, b, :], in_=spread[:])
+
+        w2_codes = keep.tile([P, PASSES * HEADS], U32, align_bytes=64)
+        w2_scales = keep.tile([P, PASSES * HEADS], U8, align_bytes=64)
+
+        def regroup_w2(first):
+            w2_grouped = w2_stage.tile([P, CHUNK * HEADS, PACK], BF16, align_bytes=64)
+            for g in range(CHUNK):
+                regroup(
+                    nc,
+                    w2_grouped[:, g * HEADS : (g + 1) * HEADS, :],
+                    w2_raw[:, first + g, :].rearrange("p (t k) -> p t k", t=PACK),
+                )
+            return w2_grouped
+
+        def quantise_w2(first, w2_grouped):
+            cols = slice(first * HEADS, (first + CHUNK) * HEADS)
+            nc.vector.quantize_mx(
+                out=w2_codes[:, cols].bitcast(FP8X4),
+                scales=w2_scales[:, cols],
+                in_=w2_grouped[:].rearrange("p w t -> p (w t)"),
+            )
+
+        quantise_w2(0, regroup_w2(0))
+
+        acc = [psum.tile([P, COLS], F32, name="acc%d" % b) for b in range(BATCH)]
+        for g in range(PASSES):
+            h_planes = planes[g % PLANE_BUFS]
+            for t in range(PACK):
+                nc.scalar.activation(
+                    out=h_planes[:, t, :, 0:USED],
+                    in_=dist[:, :, 0:USED],
+                    func=ACT.Silu,
+                    scale=affine[:, t, g : g + 1],
+                    bias=affine[:, t, PASSES + g : PASSES + g + 1],
+                )
+            h_grouped = []
+            for b in range(BATCH):
+                grouped = h_stage.tile([P, COLS, PACK], BF16, align_bytes=64, name="grouped")
+                regroup(nc, grouped[:], h_planes[:, :, b, :])
+                h_grouped.append(grouped)
+            next_chunk = g + CHUNK if g % CHUNK == 0 and g + CHUNK < PASSES else None
+            if next_chunk is not None:
+                w2_grouped = regroup_w2(next_chunk)
+            for b in range(BATCH):
+                h_codes = h_stage.tile([P, COLS], U32, align_bytes=64, name="h_codes")
+                h_scales = h_stage.tile([P, COLS], U8, align_bytes=64, name="h_scales")
+                nc.vector.quantize_mx(
+                    out=h_codes[:].bitcast(FP8X4),
+                    scales=h_scales[:],
+                    in_=h_grouped[b][:].rearrange("p w t -> p (w t)"),
+                )
+                nc.tensor.matmul_mx(
+                    out=acc[b][:],
+                    lhsT=w2_codes[:, g * HEADS : (g + 1) * HEADS].bitcast(FP8X4),
+                    lhsT_scale=w2_scales[:, g * HEADS : (g + 1) * HEADS],
+                    rhs=h_codes[:].bitcast(FP8X4),
+                    rhs_scale=h_scales[:],
+                    start=(g == 0),
+                    stop=(g == PASSES - 1),
+                )
+            if next_chunk is not None:
+                quantise_w2(next_chunk, w2_grouped)
+
+        result = keep.tile([P, BATCH, POINTS * OUT_ROW], F32)
+
+        def add_b2_on_vector(dst, src):
+            nc.vector.tensor_scalar_add(out=dst, in0=src, scalar1=b2_col[:, 0:1])
+
+        def add_b2_on_scalar(dst, src):
+            nc.scalar.activation(out=dst, in_=src, func=ACT.Identity, bias=b2_col[:, 0:1])
+
+        def expand(b, add_b2):
+            for m, offset in levels:
+                blocks = POINTS // (2 * m)
+                pairs = acc[b][:, offset : offset + blocks * m * m]
+                squares_2m = result[:, b, :].rearrange("k (q w) -> k q w", w=2 * m * OUT_ROW)
+                top = squares_2m[:, :, 0 : m * POINTS].rearrange("k q (a x) -> k q a x", x=POINTS)
+                bottom = squares_2m[:, :, m * POINTS : 2 * m * POINTS].rearrange("k q (c x) -> k q c x", x=POINTS)
+                add_b2(top[:, :, :, m : 2 * m], pairs.rearrange("k (q a c) -> k q a c", a=m, c=m))
+                add_b2(bottom[:, :, :, 0:m], pairs.rearrange("k (q a c) -> k q c a", a=m, c=m))
+            add_b2(
+                result[:, b, :].rearrange("k (i w) -> k i w", w=OUT_ROW)[:, :, 0:1],
+                acc[b][:, PAIRS:USED].unsqueeze(1).to_broadcast([P, POINTS, 1]),
+            )
+
+        expand(0, add_b2_on_vector)
+        expand(1, add_b2_on_scalar)
+        for b in range(BATCH):
+            nc.sync.dma_start(out=out[b].rearrange("k i j -> k (i j)"), in_=result[:, b, 0 : POINTS * POINTS])

@@ -29,6 +29,7 @@ PART_COLS = COLS // P
 CHUNK = 4
 RUN = 4
 PLANE_BUFS = 3
+TAIL_PASSES = 2
 OUT_ROW = POINTS + 1
 
 FLOPS = 2 * BATCH * POINTS * POINTS * HIDDEN * HEADS
@@ -87,7 +88,7 @@ def tile_distancerelativebias_k_kernel(tc, coords, w1, b1, w2, b2, out):
         warm_sqrt = keep.tile([P, 1], F32)
         nc.scalar.activation(out=warm_sqrt[:], in_=one[:], func=ACT.Sqrt)
 
-        planes = [keep.tile([P, PACK, BATCH, COLS], BF16, name="planes%d" % r) for r in range(PLANE_BUFS)]
+        planes = [keep.tile([P, BATCH, PACK, COLS], BF16, name="planes%d" % r) for r in range(PLANE_BUFS)]
         for r in range(PLANE_BUFS):
             nc.gpsimd.memset(planes[r][:, :, :, PAIRS:COLS], 0.0)
 
@@ -164,43 +165,50 @@ def tile_distancerelativebias_k_kernel(tc, coords, w1, b1, w2, b2, out):
         quantise_w2(0, regroup_w2(0))
 
         acc = [psum.tile([P, COLS], F32, name="acc%d" % b) for b in range(BATCH)]
-        for g in range(PASSES):
-            h_planes = planes[g % PLANE_BUFS]
+
+        def silu(g, batches):
             for t in range(PACK):
                 nc.scalar.activation(
-                    out=h_planes[:, t, :, 0:USED],
-                    in_=dist[:, :, 0:USED],
+                    out=planes[g % PLANE_BUFS][:, batches, t, 0:USED],
+                    in_=dist[:, batches, 0:USED],
                     func=ACT.Silu,
                     scale=affine[:, t, g : g + 1],
                     bias=affine[:, t, PASSES + g : PASSES + g + 1],
                 )
-            h_grouped = []
-            for b in range(BATCH):
-                grouped = h_stage.tile([P, COLS, PACK], BF16, align_bytes=64, name="grouped")
-                regroup(nc, grouped[:], h_planes[:, :, b, :])
-                h_grouped.append(grouped)
-            next_chunk = g + CHUNK if g % CHUNK == 0 and g + CHUNK < PASSES else None
-            if next_chunk is not None:
-                w2_grouped = regroup_w2(next_chunk)
-            for b in range(BATCH):
-                h_codes = h_stage.tile([P, COLS], U32, align_bytes=64, name="h_codes")
-                h_scales = h_stage.tile([P, COLS], U8, align_bytes=64, name="h_scales")
-                nc.vector.quantize_mx(
-                    out=h_codes[:].bitcast(FP8X4),
-                    scales=h_scales[:],
-                    in_=h_grouped[b][:].rearrange("p w t -> p (w t)"),
-                )
-                nc.tensor.matmul_mx(
-                    out=acc[b][:],
-                    lhsT=w2_codes[:, g * HEADS : (g + 1) * HEADS].bitcast(FP8X4),
-                    lhsT_scale=w2_scales[:, g * HEADS : (g + 1) * HEADS],
-                    rhs=h_codes[:].bitcast(FP8X4),
-                    rhs_scale=h_scales[:],
-                    start=(g == 0),
-                    stop=(g == PASSES - 1),
-                )
-            if next_chunk is not None:
-                quantise_w2(next_chunk, w2_grouped)
+
+        def regroup_h(g, b):
+            grouped = h_stage.tile([P, COLS, PACK], BF16, align_bytes=64)
+            regroup(nc, grouped[:], planes[g % PLANE_BUFS][:, b, :, :])
+            return grouped
+
+        def quantise_and_multiply(g, b, grouped):
+            h_codes = h_stage.tile([P, COLS], U32, align_bytes=64)
+            h_scales = h_stage.tile([P, COLS], U8, align_bytes=64)
+            nc.vector.quantize_mx(
+                out=h_codes[:].bitcast(FP8X4), scales=h_scales[:], in_=grouped[:].rearrange("p w t -> p (w t)")
+            )
+            nc.tensor.matmul_mx(
+                out=acc[b][:],
+                lhsT=w2_codes[:, g * HEADS : (g + 1) * HEADS].bitcast(FP8X4),
+                lhsT_scale=w2_scales[:, g * HEADS : (g + 1) * HEADS],
+                rhs=h_codes[:].bitcast(FP8X4),
+                rhs_scale=h_scales[:],
+                start=(g == 0),
+                stop=(g == PASSES - 1),
+            )
+
+        for g in range(PASSES):
+            if g == 0 or g >= PASSES - TAIL_PASSES:
+                for b in range(BATCH):
+                    silu(g, slice(b, b + 1))
+                    quantise_and_multiply(g, b, regroup_h(g, b))
+            else:
+                silu(g, slice(0, BATCH))
+                h_grouped = [regroup_h(g, b) for b in range(BATCH)]
+                for b in range(BATCH):
+                    quantise_and_multiply(g, b, h_grouped[b])
+            if g % CHUNK == 0 and g + CHUNK < PASSES:
+                quantise_w2(g + CHUNK, regroup_w2(g + CHUNK))
 
         result = keep.tile([P, BATCH, POINTS * OUT_ROW], F32)
 

@@ -29,7 +29,7 @@ PART_COLS = COLS // P
 CHUNK = 4
 RUN = 4
 PLANE_BUFS = 3
-TAIL_PASSES = 2
+TAIL_PASSES = 3
 OUT_ROW = POINTS + 1
 
 FLOPS = 2 * BATCH * POINTS * POINTS * HIDDEN * HEADS
@@ -232,7 +232,7 @@ def tile_distancerelativebias_k_kernel(tc, coords, w1, b1, w2, b2, out):
                 acc[b][:, PAIRS:USED].unsqueeze(1).to_broadcast([P, POINTS, 1]),
             )
 
-        expand(0, add_b2_on_vector)
-        expand(1, add_b2_on_scalar)
+        expand(0, add_b2_on_scalar)
+        expand(1, add_b2_on_vector)
         for b in range(BATCH):
             nc.sync.dma_start(out=out[b].rearrange("k i j -> k (i j)"), in_=result[:, b, 0 : POINTS * POINTS])

@@ -24,28 +24,29 @@ K_PASS = P * PACK
 PASSES = HIDDEN // K_PASS
 COLS = 512
 PAIRS = POINTS * (POINTS - 1) // 2
-USED = PAIRS + 1
 PART_COLS = COLS // P
 CHUNK = 4
+CHUNK_EVERY = 3
 RUN = 4
 PLANE_BUFS = 3
-TAIL_PASSES = 3
+GROUPED_BUFS = 2
+TAIL_PASSES = 7
 OUT_ROW = POINTS + 1
 
+SEGMENTS = [
+    (16, 0, 1, 0),
+    (8, 0, 1, 256), (4, 0, 2, 320), (2, 0, 4, 352), (1, 0, 16, 368),
+    (8, 1, 1, 384), (4, 2, 2, 448), (2, 4, 4, 480),
+]
+PARTS = [(0, 256, SEGMENTS[0:1]), (256, 384, SEGMENTS[1:5]), (384, 512, SEGMENTS[5:8])]
+
+BASE = (0, PAIRS)
+DIAGONAL = 2 * PAIRS
+USED = 2 * PAIRS + 1
+MOVED = (PAIRS, PAIRS + 8)
+PLANE = BASE[1] + MOVED[1]
+
 FLOPS = 2 * BATCH * POINTS * POINTS * HIDDEN * HEADS
-
-
-def block_levels():
-    levels = []
-    offset = 0
-    m = POINTS // 2
-    while m >= 1:
-        levels.append((m, offset))
-        offset += (POINTS // (2 * m)) * m * m
-        m //= 2
-    assert offset == PAIRS
-    return levels
-
 
 def regroup(nc, grouped, planes):
     nc.vector.tensor_copy(
@@ -56,7 +57,6 @@ def regroup(nc, grouped, planes):
 
 def tile_distancerelativebias_k_kernel(tc, coords, w1, b1, w2, b2, out):
     nc = tc.nc
-    levels = block_levels()
     with ExitStack() as ctx:
         ctx.enter_context(tc.manual_schedule())
         keep = ctx.enter_context(tc.tile_pool(name="keep", bufs=1))
@@ -88,15 +88,31 @@ def tile_distancerelativebias_k_kernel(tc, coords, w1, b1, w2, b2, out):
         warm_sqrt = keep.tile([P, 1], F32)
         nc.scalar.activation(out=warm_sqrt[:], in_=one[:], func=ACT.Sqrt)
 
-        planes = [keep.tile([P, BATCH, PACK, COLS], BF16, name="planes%d" % r) for r in range(PLANE_BUFS)]
+        planes = [keep.tile([P, PACK, PLANE], BF16, name="planes%d" % r) for r in range(PLANE_BUFS)]
+        cut_planes = [
+            [keep.tile([P, PACK, MOVED[b]], BF16, name="cut%d_%d" % (b, r)) for r in range(PLANE_BUFS)]
+            for b in range(BATCH)
+        ]
+        part_planes = [
+            keep.tile([P, PACK, min(hi, PAIRS) - lo], BF16, name="part%d" % lo) for lo, hi, segments in PARTS
+        ]
         for r in range(PLANE_BUFS):
-            nc.gpsimd.memset(planes[r][:, :, :, PAIRS:COLS], 0.0)
+            nc.gpsimd.memset(planes[r][:, :, DIAGONAL:PLANE], 0.0)
+            nc.gpsimd.memset(cut_planes[1][r][:, :, PAIRS : MOVED[1]], 0.0)
+        grouped = [
+            [keep.tile([P, COLS, PACK], BF16, align_bytes=64, name="grouped%d_%d" % (b, r)) for r in range(GROUPED_BUFS)]
+            for b in range(BATCH)
+        ]
+        for b in range(BATCH):
+            for r in range(GROUPED_BUFS):
+                nc.gpsimd.memset(grouped[b][r][:, MOVED[b] : COLS, :], 0.0)
 
         pair_diff = keep.tile([P, COLS], BF16)
         nc.vector.memset(pair_diff[:, PAIRS:COLS], 0.0)
-        for m, offset in levels:
-            halves = ident_bf[:, 0:POINTS].rearrange("i (q two m) -> i q two m", two=2, m=m)
-            blocks = POINTS // (2 * m)
+        for m, first, blocks, offset in SEGMENTS:
+            halves = ident_bf[:, 2 * m * first : 2 * m * (first + blocks)].rearrange(
+                "i (q two m) -> i q two m", two=2, m=m
+            )
             nc.vector.tensor_sub(
                 out=pair_diff[:, offset : offset + blocks * m * m].rearrange("i (q a c) -> i q a c", a=m, c=m),
                 in0=halves[:, :, 0, :].unsqueeze(3).to_broadcast([P, blocks, m, m]),
@@ -132,14 +148,15 @@ def tile_distancerelativebias_k_kernel(tc, coords, w1, b1, w2, b2, out):
         b2_col = keep.tile([P, 1], F32)
         nc.vector.tensor_copy(out=b2_col[:], in_=turned[:, PACK, 2 * PASSES : 2 * PASSES + 1])
 
-        dist = keep.tile([P, BATCH, COLS], F32)
+        dist = keep.tile([P, USED], F32)
         for b in range(BATCH):
             spread = psum.tile([P, COLS], F32, name="spread%d" % b)
             for l in range(PART_COLS):
                 nc.tensor.transpose(
                     spread[:, l * P : (l + 1) * P], dist_col[:, l, b : b + 1].to_broadcast([P, P]), ident_f32[:]
                 )
-            nc.vector.tensor_copy(out=dist[:, b, :], in_=spread[:])
+            cols = USED - BASE[1] if b == 1 else PAIRS
+            nc.vector.tensor_copy(out=dist[:, BASE[b] : BASE[b] + cols], in_=spread[:, 0:cols])
 
         w2_codes = keep.tile([P, PASSES * HEADS], U32, align_bytes=64)
         w2_scales = keep.tile([P, PASSES * HEADS], U8, align_bytes=64)
@@ -164,75 +181,141 @@ def tile_distancerelativebias_k_kernel(tc, coords, w1, b1, w2, b2, out):
 
         quantise_w2(0, regroup_w2(0))
 
-        acc = [psum.tile([P, COLS], F32, name="acc%d" % b) for b in range(BATCH)]
+        acc0 = [psum.tile([P, COLS], F32, name="acc0_%d" % lo) for lo, hi, segments in PARTS]
+        acc1 = psum.tile([P, COLS], F32)
 
-        def silu(g, batches):
+        def silu(g, dst, first, last):
             for t in range(PACK):
                 nc.scalar.activation(
-                    out=planes[g % PLANE_BUFS][:, batches, t, 0:USED],
-                    in_=dist[:, batches, 0:USED],
+                    out=dst[:, t, 0 : last - first],
+                    in_=dist[:, first:last],
                     func=ACT.Silu,
                     scale=affine[:, t, g : g + 1],
                     bias=affine[:, t, PASSES + g : PASSES + g + 1],
                 )
 
-        def regroup_h(g, b):
-            grouped = h_stage.tile([P, COLS, PACK], BF16, align_bytes=64)
-            regroup(nc, grouped[:], planes[g % PLANE_BUFS][:, b, :, :])
-            return grouped
+        def silu_of_batch(g, b):
+            silu(g, cut_planes[b][g % PLANE_BUFS], BASE[b], USED if b == 1 else BASE[1])
 
-        def quantise_and_multiply(g, b, grouped):
-            h_codes = h_stage.tile([P, COLS], U32, align_bytes=64)
-            h_scales = h_stage.tile([P, COLS], U8, align_bytes=64)
+        def regroup_h(g, b, src, lo=0):
+            regroup(nc, grouped[b][g % GROUPED_BUFS][:, lo : lo + src.shape[2], :], src)
+
+        def regroup_batch(g, b):
+            regroup_h(g, b, cut_planes[b][g % PLANE_BUFS][:])
+
+        def operand():
+            codes = h_stage.tile([P, COLS], U32, align_bytes=64)
+            scales = h_stage.tile([P, COLS], U8, align_bytes=64)
+            return codes, scales
+
+        def quantise(g, b, h, lo=0, hi=COLS):
+            codes, scales = h
             nc.vector.quantize_mx(
-                out=h_codes[:].bitcast(FP8X4), scales=h_scales[:], in_=grouped[:].rearrange("p w t -> p (w t)")
+                out=codes[:, lo:hi].bitcast(FP8X4),
+                scales=scales[:, lo:hi],
+                in_=grouped[b][g % GROUPED_BUFS][:, lo:hi, :].rearrange("p w t -> p (w t)"),
             )
+
+        def multiply(g, sums, h, lo, hi):
+            codes, scales = h
             nc.tensor.matmul_mx(
-                out=acc[b][:],
+                out=sums[:, 0 : hi - lo],
                 lhsT=w2_codes[:, g * HEADS : (g + 1) * HEADS].bitcast(FP8X4),
                 lhsT_scale=w2_scales[:, g * HEADS : (g + 1) * HEADS],
-                rhs=h_codes[:].bitcast(FP8X4),
-                rhs_scale=h_scales[:],
+                rhs=codes[:, lo:hi].bitcast(FP8X4),
+                rhs_scale=scales[:, lo:hi],
                 start=(g == 0),
                 stop=(g == PASSES - 1),
             )
 
-        for g in range(PASSES):
-            if g == 0 or g >= PASSES - TAIL_PASSES:
-                for b in range(BATCH):
-                    silu(g, slice(b, b + 1))
-                    quantise_and_multiply(g, b, regroup_h(g, b))
+        def quantise_and_multiply(g, b):
+            h = operand()
+            quantise(g, b, h)
+            if b == 1:
+                multiply(g, acc1, h, 0, COLS)
             else:
-                silu(g, slice(0, BATCH))
-                h_grouped = [regroup_h(g, b) for b in range(BATCH)]
-                for b in range(BATCH):
-                    quantise_and_multiply(g, b, h_grouped[b])
-            if g % CHUNK == 0 and g + CHUNK < PASSES:
-                quantise_w2(g + CHUNK, regroup_w2(g + CHUNK))
+                for sums, (lo, hi, segments) in zip(acc0, PARTS):
+                    multiply(g, sums, h, lo, hi)
+
+        for b in range(BATCH):
+            silu_of_batch(0, b)
+            regroup_batch(0, b)
+            quantise_and_multiply(0, b)
+        for g in range(1, PASSES - TAIL_PASSES):
+            silu(g, planes[g % PLANE_BUFS], 0, USED)
+            for b in range(BATCH):
+                regroup_h(g, b, planes[g % PLANE_BUFS][:, :, BASE[b] : BASE[b] + MOVED[b]])
+            for b in range(BATCH):
+                quantise_and_multiply(g, b)
+            chunk = (g // CHUNK_EVERY + 1) * CHUNK
+            if g % CHUNK_EVERY == 1 and chunk < PASSES:
+                quantise_w2(chunk, regroup_w2(chunk))
 
         result = keep.tile([P, BATCH, POINTS * OUT_ROW], F32)
 
-        def add_b2_on_vector(dst, src):
+        def on_vector(dst, src):
             nc.vector.tensor_scalar_add(out=dst, in0=src, scalar1=b2_col[:, 0:1])
 
-        def add_b2_on_scalar(dst, src):
+        def on_scalar(dst, src):
             nc.scalar.activation(out=dst, in_=src, func=ACT.Identity, bias=b2_col[:, 0:1])
 
-        def expand(b, add_b2):
-            for m, offset in levels:
-                blocks = POINTS // (2 * m)
-                pairs = acc[b][:, offset : offset + blocks * m * m]
+        def place(b, sums, lo, segments):
+            copies = []
+            for m, first, blocks, offset in segments:
+                pairs = sums[:, offset - lo : offset - lo + blocks * m * m]
                 squares_2m = result[:, b, :].rearrange("k (q w) -> k q w", w=2 * m * OUT_ROW)
+                squares_2m = squares_2m[:, first : first + blocks, :]
                 top = squares_2m[:, :, 0 : m * POINTS].rearrange("k q (a x) -> k q a x", x=POINTS)
                 bottom = squares_2m[:, :, m * POINTS : 2 * m * POINTS].rearrange("k q (c x) -> k q c x", x=POINTS)
-                add_b2(top[:, :, :, m : 2 * m], pairs.rearrange("k (q a c) -> k q a c", a=m, c=m))
-                add_b2(bottom[:, :, :, 0:m], pairs.rearrange("k (q a c) -> k q c a", a=m, c=m))
-            add_b2(
+                copies.append((top[:, :, :, m : 2 * m], pairs.rearrange("k (q a c) -> k q a c", a=m, c=m)))
+                copies.append((bottom[:, :, :, 0:m], pairs.rearrange("k (q a c) -> k q c a", a=m, c=m)))
+            return copies
+
+        def place_diagonal(b):
+            return (
                 result[:, b, :].rearrange("k (i w) -> k i w", w=OUT_ROW)[:, :, 0:1],
-                acc[b][:, PAIRS:USED].unsqueeze(1).to_broadcast([P, POINTS, 1]),
+                acc1[:, PAIRS : PAIRS + 1].unsqueeze(1).to_broadcast([P, POINTS, 1]),
             )
 
-        expand(0, add_b2_on_scalar)
-        expand(1, add_b2_on_vector)
-        for b in range(BATCH):
-            nc.sync.dma_start(out=out[b].rearrange("k i j -> k (i j)"), in_=result[:, b, 0 : POINTS * POINTS])
+        def store(b, first, last):
+            nc.sync.dma_start(
+                out=out[b, :, first:last, :].rearrange("k i j -> k (i j)"),
+                in_=result[:, b, first * POINTS : last * POINTS],
+            )
+
+        tail = range(PASSES - TAIL_PASSES, PASSES)
+        for g in tail:
+            silu_of_batch(g, 1)
+            regroup_batch(g, 1)
+            quantise_and_multiply(g, 1)
+        copies = place(1, acc1, 0, SEGMENTS) + [place_diagonal(1), place_diagonal(0)]
+        share = -(-len(copies) // (TAIL_PASSES - 1))
+        for n, g in enumerate(tail[:-1]):
+            silu_of_batch(g, 0)
+            regroup_batch(g, 0)
+            for dst, src in copies[n * share : (n + 1) * share]:
+                on_vector(dst, src)
+            quantise_and_multiply(g, 0)
+        store(1, 0, POINTS)
+        g = PASSES - 1
+        h = operand()
+        for plane, (lo, hi, segments) in zip(part_planes, PARTS):
+            silu(g, plane, lo, min(hi, PAIRS))
+        (a_lo, a_hi, a_segments), (b_lo, b_hi, b_segments), (c_lo, c_hi, c_segments) = PARTS
+        regroup_h(g, 0, part_planes[0][:], a_lo)
+        regroup_h(g, 0, part_planes[1][:], b_lo)
+        quantise(g, 0, h, a_lo, a_hi)
+        multiply(g, acc0[0], h, a_lo, a_hi)
+        regroup_h(g, 0, part_planes[2][:], c_lo)
+        quantise(g, 0, h, b_lo, b_hi)
+        multiply(g, acc0[1], h, b_lo, b_hi)
+        quantise(g, 0, h, c_lo, c_hi)
+        multiply(g, acc0[2], h, c_lo, c_hi)
+        for dst, src in place(0, acc0[0], a_lo, a_segments):
+            on_scalar(dst, src)
+        for dst, src in place(0, acc0[1], b_lo, b_segments):
+            on_vector(dst, src)
+        store(0, 0, POINTS // 2)
+        for dst, src in place(0, acc0[2], c_lo, c_segments):
+            on_scalar(dst, src)
+        store(0, POINTS // 2, POINTS)

@@ -33,12 +33,11 @@ GROUPED_BUFS = 2
 TAIL_PASSES = 7
 OUT_ROW = POINTS + 1
 
-SEGMENTS = [
-    (16, 0, 1, 0),
-    (8, 0, 1, 256), (4, 0, 2, 320), (2, 0, 4, 352), (1, 0, 16, 368),
-    (8, 1, 1, 384), (4, 2, 2, 448), (2, 4, 4, 480),
-]
-PARTS = [(0, 256, SEGMENTS[0:1]), (256, 384, SEGMENTS[1:5]), (384, 512, SEGMENTS[5:8])]
+SEGMENTS = [(16, 0, 1, 0), (8, 0, 2, 256), (4, 0, 4, 384), (2, 0, 8, 448), (1, 0, 16, 480)]
+PARTS = [(0, 256, SEGMENTS[0:1]), (384, 512, SEGMENTS[2:5]), (256, 384, SEGMENTS[1:2])]
+
+LAST_WINDOWS = ([(0, 256), (256, 512)], [(lo, hi) for lo, hi, segments in PARTS])
+COPIES_PER_JOB = 3
 
 BASE = (0, PAIRS)
 DIAGONAL = 2 * PAIRS
@@ -65,7 +64,8 @@ def tile_distancerelativebias_k_kernel(tc, coords, w1, b1, w2, b2, out):
         psum = ctx.enter_context(tc.psum_pool(name="psum", bufs=1))
 
         points = keep.tile([P, BATCH, DIM], BF16)
-        nc.vector.memset(points[:], 0.0)
+        nc.vector.memset(points[POINTS : 2 * POINTS, :, :], 0.0)
+        nc.vector.memset(points[2 * POINTS : P, :, :], 0.0)
         nc.sync.dma_start(out=points[0:POINTS, :, :], in_=coords.rearrange("b i c -> i b c"))
         rows = keep.tile([P, K_PASS], BF16)
         nc.vector.memset(rows[2 * PASSES : P, :], 0.0)
@@ -94,7 +94,8 @@ def tile_distancerelativebias_k_kernel(tc, coords, w1, b1, w2, b2, out):
             for b in range(BATCH)
         ]
         part_planes = [
-            keep.tile([P, PACK, min(hi, PAIRS) - lo], BF16, name="part%d" % lo) for lo, hi, segments in PARTS
+            [keep.tile([P, PACK, min(hi, PAIRS) - lo], BF16, name="part%d_%d" % (r, lo)) for lo, hi in windows]
+            for r, windows in enumerate(LAST_WINDOWS)
         ]
         for r in range(PLANE_BUFS):
             nc.gpsimd.memset(planes[r][:, :, DIAGONAL:PLANE], 0.0)
@@ -149,14 +150,18 @@ def tile_distancerelativebias_k_kernel(tc, coords, w1, b1, w2, b2, out):
         nc.vector.tensor_copy(out=b2_col[:], in_=turned[:, PACK, 2 * PASSES : 2 * PASSES + 1])
 
         dist = keep.tile([P, USED], F32)
+        spread = [psum.tile([P, COLS], F32, name="spread%d" % b) for b in range(BATCH)]
         for b in range(BATCH):
-            spread = psum.tile([P, COLS], F32, name="spread%d" % b)
             for l in range(PART_COLS):
                 nc.tensor.transpose(
-                    spread[:, l * P : (l + 1) * P], dist_col[:, l, b : b + 1].to_broadcast([P, P]), ident_f32[:]
+                    spread[b][:, l * P : (l + 1) * P], dist_col[:, l, b : b + 1].to_broadcast([P, P]), ident_f32[:]
                 )
-            cols = USED - BASE[1] if b == 1 else PAIRS
-            nc.vector.tensor_copy(out=dist[:, BASE[b] : BASE[b] + cols], in_=spread[:, 0:cols])
+
+        def copy_dist(b):
+            cols = PAIRS + b
+            nc.vector.tensor_copy(out=dist[:, BASE[b] : BASE[b] + cols], in_=spread[b][:, 0:cols])
+
+        copy_dist(1)
 
         w2_codes = keep.tile([P, PASSES * HEADS], U32, align_bytes=64)
         w2_scales = keep.tile([P, PASSES * HEADS], U8, align_bytes=64)
@@ -184,18 +189,15 @@ def tile_distancerelativebias_k_kernel(tc, coords, w1, b1, w2, b2, out):
         acc0 = [psum.tile([P, COLS], F32, name="acc0_%d" % lo) for lo, hi, segments in PARTS]
         acc1 = psum.tile([P, COLS], F32)
 
-        def silu(g, dst, first, last):
+        def silu(g, dst, src):
             for t in range(PACK):
                 nc.scalar.activation(
-                    out=dst[:, t, 0 : last - first],
-                    in_=dist[:, first:last],
+                    out=dst[:, t, 0 : src.shape[1]],
+                    in_=src,
                     func=ACT.Silu,
                     scale=affine[:, t, g : g + 1],
                     bias=affine[:, t, PASSES + g : PASSES + g + 1],
                 )
-
-        def silu_of_batch(g, b):
-            silu(g, cut_planes[b][g % PLANE_BUFS], BASE[b], USED if b == 1 else BASE[1])
 
         def regroup_h(g, b, src, lo=0):
             regroup(nc, grouped[b][g % GROUPED_BUFS][:, lo : lo + src.shape[2], :], src)
@@ -238,11 +240,15 @@ def tile_distancerelativebias_k_kernel(tc, coords, w1, b1, w2, b2, out):
                     multiply(g, sums, h, lo, hi)
 
         for b in range(BATCH):
-            silu_of_batch(0, b)
+            if b == 0:
+                silu(0, cut_planes[b][0], spread[b][:, 0:PAIRS])
+                copy_dist(b)
+            else:
+                silu(0, cut_planes[b][0], dist[:, BASE[b] : USED])
             regroup_batch(0, b)
             quantise_and_multiply(0, b)
         for g in range(1, PASSES - TAIL_PASSES):
-            silu(g, planes[g % PLANE_BUFS], 0, USED)
+            silu(g, planes[g % PLANE_BUFS], dist[:])
             for b in range(BATCH):
                 regroup_h(g, b, planes[g % PLANE_BUFS][:, :, BASE[b] : BASE[b] + MOVED[b]])
             for b in range(BATCH):
@@ -271,51 +277,54 @@ def tile_distancerelativebias_k_kernel(tc, coords, w1, b1, w2, b2, out):
                 copies.append((bottom[:, :, :, 0:m], pairs.rearrange("k (q a c) -> k q c a", a=m, c=m)))
             return copies
 
-        def place_diagonal(b):
+        def place_diagonals():
             return (
-                result[:, b, :].rearrange("k (i w) -> k i w", w=OUT_ROW)[:, :, 0:1],
-                acc1[:, PAIRS : PAIRS + 1].unsqueeze(1).to_broadcast([P, POINTS, 1]),
+                result[:].rearrange("k b (i w) -> k b i w", w=OUT_ROW)[:, :, :, 0],
+                acc1[:, PAIRS : PAIRS + 1].unsqueeze(1).to_broadcast([P, BATCH, POINTS]),
             )
 
-        def store(b, first, last):
-            nc.sync.dma_start(
-                out=out[b, :, first:last, :].rearrange("k i j -> k (i j)"),
-                in_=result[:, b, first * POINTS : last * POINTS],
-            )
+        def store(b):
+            nc.sync.dma_start(out=out[b].rearrange("k i j -> k (i j)"), in_=result[:, b, 0 : POINTS * POINTS])
 
-        tail = range(PASSES - TAIL_PASSES, PASSES)
-        for g in tail:
-            silu_of_batch(g, 1)
-            regroup_batch(g, 1)
-            quantise_and_multiply(g, 1)
-        copies = place(1, acc1, 0, SEGMENTS) + [place_diagonal(1), place_diagonal(0)]
-        share = -(-len(copies) // (TAIL_PASSES - 1))
-        for n, g in enumerate(tail[:-1]):
-            silu_of_batch(g, 0)
-            regroup_batch(g, 0)
-            for dst, src in copies[n * share : (n + 1) * share]:
-                on_vector(dst, src)
-            quantise_and_multiply(g, 0)
-        store(1, 0, POINTS)
-        g = PASSES - 1
-        h = operand()
-        for plane, (lo, hi, segments) in zip(part_planes, PARTS):
-            silu(g, plane, lo, min(hi, PAIRS))
-        (a_lo, a_hi, a_segments), (b_lo, b_hi, b_segments), (c_lo, c_hi, c_segments) = PARTS
-        regroup_h(g, 0, part_planes[0][:], a_lo)
-        regroup_h(g, 0, part_planes[1][:], b_lo)
-        quantise(g, 0, h, a_lo, a_hi)
-        multiply(g, acc0[0], h, a_lo, a_hi)
-        regroup_h(g, 0, part_planes[2][:], c_lo)
-        quantise(g, 0, h, b_lo, b_hi)
-        multiply(g, acc0[1], h, b_lo, b_hi)
-        quantise(g, 0, h, c_lo, c_hi)
-        multiply(g, acc0[2], h, c_lo, c_hi)
-        for dst, src in place(0, acc0[0], a_lo, a_segments):
-            on_scalar(dst, src)
-        for dst, src in place(0, acc0[1], b_lo, b_segments):
-            on_vector(dst, src)
-        store(0, 0, POINTS // 2)
-        for dst, src in place(0, acc0[2], c_lo, c_segments):
-            on_scalar(dst, src)
-        store(0, POINTS // 2, POINTS)
+        jobs = []
+        for g in range(PASSES - TAIL_PASSES, PASSES):
+            jobs.append((g, 1, cut_planes[1][g % PLANE_BUFS], 0, COLS))
+        for g in range(PASSES - TAIL_PASSES, PASSES - 2):
+            jobs.append((g, 0, cut_planes[0][g % PLANE_BUFS], 0, COLS))
+        for g in (PASSES - 2, PASSES - 1):
+            for plane, (lo, hi) in zip(part_planes[g % 2], LAST_WINDOWS[g % 2]):
+                jobs.append((g, 0, plane, lo, hi))
+        copies = place(1, acc1, 0, SEGMENTS) + [place_diagonals()]
+        operands = {}
+        waiting = []
+
+        def finish(g, b, lo, hi):
+            if (g, b) not in operands:
+                operands[g, b] = operand()
+            quantise(g, b, operands[g, b], lo, hi)
+            if b == 1:
+                multiply(g, acc1, operands[g, b], lo, hi)
+            else:
+                for sums, (first, last, segments) in zip(acc0, PARTS):
+                    if lo <= first and last <= hi:
+                        multiply(g, sums, operands[g, b], first, last)
+
+        for n, (g, b, plane, lo, hi) in enumerate(jobs):
+            silu(g, plane, dist[:, BASE[b] + lo : BASE[b] + min(hi, PAIRS + b)])
+            regroup_h(g, b, plane[:], lo)
+            for job in waiting:
+                finish(*job)
+            waiting = [(g, b, lo, hi)]
+            if b == 0:
+                if n > TAIL_PASSES:
+                    for dst, src in copies[:COPIES_PER_JOB]:
+                        on_vector(dst, src)
+                    copies = copies[COPIES_PER_JOB:]
+                finish(*waiting.pop())
+        assert not copies
+        store(1)
+        add_b2 = (on_scalar, on_vector, on_scalar)
+        for sums, (lo, hi, segments), add in zip(acc0, PARTS, add_b2):
+            for dst, src in place(0, sums, lo, segments):
+                add(dst, src)
+        store(0)

@@ -298,10 +298,11 @@ def tile_distancerelativebias_k_kernel(tc, coords, w1, b1, w2, b2, out):
         operands = {}
         waiting = []
 
-        def finish(g, b, lo, hi):
+        def finish(g, b, lo, hi, pieces):
             if (g, b) not in operands:
                 operands[g, b] = operand()
-            quantise(g, b, operands[g, b], lo, hi)
+            for first, last in pieces:
+                quantise(g, b, operands[g, b], first, last)
             if b == 1:
                 multiply(g, acc1, operands[g, b], lo, hi)
             else:
@@ -309,12 +310,18 @@ def tile_distancerelativebias_k_kernel(tc, coords, w1, b1, w2, b2, out):
                     if lo <= first and last <= hi:
                         multiply(g, sums, operands[g, b], first, last)
 
+        def halves(lo, hi):
+            mid = (lo + hi) // 2
+            return [(lo, mid), (mid, hi)] if hi - lo >= 256 else [(lo, hi)]
+
         for n, (g, b, plane, lo, hi) in enumerate(jobs):
             silu(g, plane, dist[:, BASE[b] + lo : BASE[b] + min(hi, PAIRS + b)])
-            regroup_h(g, b, plane[:], lo)
+            pieces = halves(lo, hi) if b == 0 else [(lo, hi)]
+            for first, last in pieces:
+                regroup_h(g, b, plane[:, :, first - lo : min(last - lo, plane.shape[2])], first)
             for job in waiting:
                 finish(*job)
-            waiting = [(g, b, lo, hi)]
+            waiting = [(g, b, lo, hi, pieces)]
             if b == 0:
                 if n > TAIL_PASSES:
                     for dst, src in copies[:COPIES_PER_JOB]:

@@ -68,10 +68,12 @@ def tile_distancerelativebias_k_kernel(tc, coords, w1, b1, w2, b2, out):
         nc.vector.memset(points[2 * POINTS : P, :, :], 0.0)
         nc.sync.dma_start(out=points[0:POINTS, :, :], in_=coords.rearrange("b i c -> i b c"))
         rows = keep.tile([P, K_PASS], BF16)
+        nc.scalar.dma_start(out=rows[0:PASSES, :], in_=w1.rearrange("o (g x) -> (o g) x", x=K_PASS))
+        nc.scalar.dma_start(out=rows[PASSES : 2 * PASSES, :], in_=b1.rearrange("(g x) -> g x", x=K_PASS))
         nc.vector.memset(rows[2 * PASSES : P, :], 0.0)
-        nc.sync.dma_start(out=rows[0:PASSES, :], in_=w1.rearrange("o (g x) -> (o g) x", x=K_PASS))
-        nc.sync.dma_start(out=rows[PASSES : 2 * PASSES, :], in_=b1.rearrange("(g x) -> g x", x=K_PASS))
-        nc.sync.dma_start(out=rows[2 * PASSES : 2 * PASSES + 1, 0:HEADS], in_=b2.rearrange("(o k) -> o k", o=1))
+        b2_row = keep.tile([P, P], BF16)
+        nc.vector.memset(b2_row[:], 0.0)
+        nc.sync.dma_start(out=b2_row[0:1, 0:HEADS], in_=b2.rearrange("(o k) -> o k", o=1))
         w2_raw = keep.tile([P, PASSES, PACK * HEADS], BF16)
         for first in range(0, PASSES, CHUNK):
             nc.sync.dma_start(
@@ -138,16 +140,13 @@ def tile_distancerelativebias_k_kernel(tc, coords, w1, b1, w2, b2, out):
         dist_col = keep.tile([P, PART_COLS, BATCH], F32)
         nc.scalar.activation(out=dist_col[:], in_=sq_dist[:], func=ACT.Sqrt)
         warm_silu = keep.tile([P, 1], F32)
-        nc.scalar.activation(out=warm_silu[:], in_=dist_col[:, 0, 0:1], func=ACT.Silu)
+        nc.scalar.activation(out=warm_silu[:], in_=one[:], func=ACT.Silu)
 
         turned = psum.tile([P, PACK + 1, P], BF16)
         for t in range(PACK):
             nc.tensor.transpose(turned[:, t, :], rows[:].rearrange("r (p t) -> r t p", t=PACK)[:, t, :], ident_bf[:])
-        nc.tensor.transpose(turned[:, PACK, :], rows[:, 0:P], ident_bf[:])
         affine = keep.tile([P, PACK, 2 * PASSES], F32)
         nc.vector.tensor_copy(out=affine[:], in_=turned[:, 0:PACK, 0 : 2 * PASSES])
-        b2_col = keep.tile([P, 1], F32)
-        nc.vector.tensor_copy(out=b2_col[:], in_=turned[:, PACK, 2 * PASSES : 2 * PASSES + 1])
 
         dist = keep.tile([P, USED], F32)
         spread = [psum.tile([P, COLS], F32, name="spread%d" % b) for b in range(BATCH)]
@@ -156,6 +155,9 @@ def tile_distancerelativebias_k_kernel(tc, coords, w1, b1, w2, b2, out):
                 nc.tensor.transpose(
                     spread[b][:, l * P : (l + 1) * P], dist_col[:, l, b : b + 1].to_broadcast([P, P]), ident_f32[:]
                 )
+
+        nc.tensor.transpose(turned[:, PACK, :], b2_row[:], ident_bf[:])
+        b2_col = keep.tile([P, 1], F32)
 
         def copy_dist(b):
             cols = PAIRS + b
@@ -256,6 +258,8 @@ def tile_distancerelativebias_k_kernel(tc, coords, w1, b1, w2, b2, out):
             chunk = (g // CHUNK_EVERY + 1) * CHUNK
             if g % CHUNK_EVERY == 1 and chunk < PASSES:
                 quantise_w2(chunk, regroup_w2(chunk))
+
+        nc.vector.tensor_copy(out=b2_col[:], in_=turned[:, PACK, 0:1])
 
         result = keep.tile([P, BATCH, POINTS * OUT_ROW], F32)
 

@@ -33,11 +33,16 @@ GROUPED_BUFS = 2
 TAIL_PASSES = 7
 OUT_ROW = POINTS + 1
 
-SEGMENTS = [(16, 0, 1, 0), (8, 0, 2, 256), (4, 0, 4, 384), (2, 0, 8, 448), (1, 0, 16, 480)]
-PARTS = [(0, 256, SEGMENTS[0:1]), (384, 512, SEGMENTS[2:5]), (256, 384, SEGMENTS[1:2])]
+RECTANGLE = [(16, 0, 1, 0, 256)]
+FIRST_SQUARE = [(8, 0, 1, 256, 64), (4, 0, 2, 320, 16), (2, 0, 4, 352, 4)]
+SINGLE = [(1, 0, 16, 368, 1)]
+SECOND_SQUARE = [(8, 1, 1, 384, 64), (4, 2, 2, 448, 16), (2, 4, 4, 480, 4)]
+SEGMENTS = RECTANGLE + FIRST_SQUARE + SINGLE + SECOND_SQUARE
+JOINED = RECTANGLE + [(8, 0, 2, 256, 128)] + FIRST_SQUARE[1:] + SINGLE + SECOND_SQUARE[1:]
+PARTS = [(0, 256, RECTANGLE), (256, 384, FIRST_SQUARE + SINGLE), (384, 512, SECOND_SQUARE)]
 
 LAST_WINDOWS = ([(0, 256), (256, 512)], [(lo, hi) for lo, hi, segments in PARTS])
-COPIES_PER_JOB = 3
+COPIES_PER_JOB = 4
 
 BASE = (0, PAIRS)
 DIAGONAL = 2 * PAIRS
@@ -112,7 +117,7 @@ def tile_distancerelativebias_k_kernel(tc, coords, w1, b1, w2, b2, out):
 
         pair_diff = keep.tile([P, COLS], BF16)
         nc.vector.memset(pair_diff[:, PAIRS:COLS], 0.0)
-        for m, first, blocks, offset in SEGMENTS:
+        for m, first, blocks, offset, stride in SEGMENTS:
             halves = ident_bf[:, 2 * m * first : 2 * m * (first + blocks)].rearrange(
                 "i (q two m) -> i q two m", two=2, m=m
             )
@@ -271,14 +276,15 @@ def tile_distancerelativebias_k_kernel(tc, coords, w1, b1, w2, b2, out):
 
         def place(b, sums, lo, segments):
             copies = []
-            for m, first, blocks, offset in segments:
-                pairs = sums[:, offset - lo : offset - lo + blocks * m * m]
+            for m, first, blocks, offset, stride in segments:
+                pairs = sums[:, offset - lo : offset - lo + blocks * stride].rearrange("k (q s) -> k q s", s=stride)
+                pairs = pairs[:, :, 0 : m * m]
                 squares_2m = result[:, b, :].rearrange("k (q w) -> k q w", w=2 * m * OUT_ROW)
                 squares_2m = squares_2m[:, first : first + blocks, :]
                 top = squares_2m[:, :, 0 : m * POINTS].rearrange("k q (a x) -> k q a x", x=POINTS)
                 bottom = squares_2m[:, :, m * POINTS : 2 * m * POINTS].rearrange("k q (c x) -> k q c x", x=POINTS)
-                copies.append((top[:, :, :, m : 2 * m], pairs.rearrange("k (q a c) -> k q a c", a=m, c=m)))
-                copies.append((bottom[:, :, :, 0:m], pairs.rearrange("k (q a c) -> k q c a", a=m, c=m)))
+                copies.append((top[:, :, :, m : 2 * m], pairs.rearrange("k q (a c) -> k q a c", a=m)))
+                copies.append((bottom[:, :, :, 0:m], pairs.rearrange("k q (a c) -> k q c a", a=m)))
             return copies
 
         def place_diagonals():
@@ -287,8 +293,11 @@ def tile_distancerelativebias_k_kernel(tc, coords, w1, b1, w2, b2, out):
                 acc1[:, PAIRS : PAIRS + 1].unsqueeze(1).to_broadcast([P, BATCH, POINTS]),
             )
 
-        def store(b):
-            nc.sync.dma_start(out=out[b].rearrange("k i j -> k (i j)"), in_=result[:, b, 0 : POINTS * POINTS])
+        def store(b, first=0, last=POINTS):
+            nc.sync.dma_start(
+                out=out[b, :, first:last, :].rearrange("k i j -> k (i j)"),
+                in_=result[:, b, first * POINTS : last * POINTS],
+            )
 
         jobs = []
         for g in range(PASSES - TAIL_PASSES, PASSES):
@@ -298,7 +307,7 @@ def tile_distancerelativebias_k_kernel(tc, coords, w1, b1, w2, b2, out):
         for g in (PASSES - 2, PASSES - 1):
             for plane, (lo, hi) in zip(part_planes[g % 2], LAST_WINDOWS[g % 2]):
                 jobs.append((g, 0, plane, lo, hi))
-        copies = place(1, acc1, 0, SEGMENTS) + [place_diagonals()]
+        copies = place(1, acc1, 0, JOINED) + [place_diagonals()]
         operands = {}
         waiting = []
 
@@ -334,8 +343,11 @@ def tile_distancerelativebias_k_kernel(tc, coords, w1, b1, w2, b2, out):
                 finish(*waiting.pop())
         assert not copies
         store(1)
-        add_b2 = (on_scalar, on_vector, on_scalar)
-        for sums, (lo, hi, segments), add in zip(acc0, PARTS, add_b2):
-            for dst, src in place(0, sums, lo, segments):
-                add(dst, src)
-        store(0)
+        for dst, src in place(0, acc0[0], PARTS[0][0], PARTS[0][2]):
+            on_scalar(dst, src)
+        for dst, src in place(0, acc0[1], PARTS[1][0], PARTS[1][2]):
+            on_vector(dst, src)
+        store(0, 0, POINTS // 2)
+        for dst, src in place(0, acc0[2], PARTS[2][0], PARTS[2][2]):
+            on_scalar(dst, src)
+        store(0, POINTS // 2, POINTS)

from contextlib import ExitStack

import concourse.mybir as mybir
from concourse.masks import make_identity

F32 = mybir.dt.float32
BF16 = mybir.dt.bfloat16
U32 = mybir.dt.uint32
U8 = mybir.dt.uint8
FP8X4 = mybir.dt.float8_e4m3fn_x4
ACT = mybir.ActivationFunctionType
ALU = mybir.AluOpType
AXIS = mybir.AxisListType

BATCH = 2
POINTS = 32
DIM = 3
HIDDEN = 16384
HEADS = 128

P = 128
PACK = 4
K_PASS = P * PACK
PASSES = HIDDEN // K_PASS
COLS = 512
PAIRS = POINTS * (POINTS - 1) // 2
PART_COLS = COLS // P
CHUNK = 4
CHUNK_EVERY = 3
RUN = 4
PLANE_BUFS = 3
GROUPED_BUFS = 2
TAIL_PASSES = 7
OUT_ROW = POINTS + 1

RECTANGLE = [(16, 0, 1, 0, 256)]
FIRST_SQUARE = [(8, 0, 1, 256, 64), (4, 0, 2, 320, 16), (2, 0, 4, 352, 4)]
SINGLE = [(1, 0, 16, 368, 1)]
SECOND_SQUARE = [(8, 1, 1, 384, 64), (4, 2, 2, 448, 16), (2, 4, 4, 480, 4)]
SEGMENTS = RECTANGLE + FIRST_SQUARE + SINGLE + SECOND_SQUARE
JOINED = RECTANGLE + [(8, 0, 2, 256, 128)] + FIRST_SQUARE[1:] + SINGLE + SECOND_SQUARE[1:]
PARTS = [(0, 256, RECTANGLE), (256, 384, FIRST_SQUARE + SINGLE), (384, 512, SECOND_SQUARE)]

LAST_WINDOWS = ([(0, 256), (256, 512)], [(lo, hi) for lo, hi, segments in PARTS])
COPIES_PER_JOB = 4

BASE = (0, PAIRS)
DIAGONAL = 2 * PAIRS
USED = 2 * PAIRS + 1
MOVED = (PAIRS, PAIRS + 8)
PLANE = BASE[1] + MOVED[1]

FLOPS = 2 * BATCH * POINTS * POINTS * HIDDEN * HEADS

def regroup(nc, grouped, planes):
    nc.vector.tensor_copy(
        out=grouped.rearrange("p (c i) t -> p c t i", i=RUN),
        in_=planes.rearrange("p t (c i) -> p c t i", i=RUN),
    )


def tile_distancerelativebias_k_kernel(tc, coords, w1, b1, w2, b2, out):
    nc = tc.nc
    with ExitStack() as ctx:
        ctx.enter_context(tc.manual_schedule())
        keep = ctx.enter_context(tc.tile_pool(name="keep", bufs=1))
        w2_stage = ctx.enter_context(tc.tile_pool(name="w2_stage", bufs=2))
        h_stage = ctx.enter_context(tc.tile_pool(name="h_stage", bufs=4))
        psum = ctx.enter_context(tc.psum_pool(name="psum", bufs=1))

        points = keep.tile([P, BATCH, DIM], BF16)
        nc.vector.memset(points[POINTS : 2 * POINTS, :, :], 0.0)
        nc.vector.memset(points[2 * POINTS : P, :, :], 0.0)
        nc.sync.dma_start(out=points[0:POINTS, :, :], in_=coords.rearrange("b i c -> i b c"))
        rows = keep.tile([P, K_PASS], BF16)
        nc.scalar.dma_start(out=rows[0:PASSES, :], in_=w1.rearrange("o (g x) -> (o g) x", x=K_PASS))
        nc.scalar.dma_start(out=rows[PASSES : 2 * PASSES, :], in_=b1.rearrange("(g x) -> g x", x=K_PASS))
        nc.vector.memset(rows[2 * PASSES : P, :], 0.0)
        b2_row = keep.tile([P, P], BF16)
        nc.vector.memset(b2_row[:], 0.0)
        nc.sync.dma_start(out=b2_row[0:1, 0:HEADS], in_=b2.rearrange("(o k) -> o k", o=1))
        w2_raw = keep.tile([P, PASSES, PACK * HEADS], BF16)
        for first in range(0, PASSES, CHUNK):
            nc.sync.dma_start(
                out=w2_raw[:, first : first + CHUNK, :],
                in_=w2[first * K_PASS : (first + CHUNK) * K_PASS, :].rearrange("(g p t) k -> p g (t k)", p=P, t=PACK),
            )

        ident_bf = keep.tile([P, P], BF16)
        make_identity(nc, ident_bf[:])
        ident_f32 = keep.tile([P, P], F32)
        make_identity(nc, ident_f32[:])
        one = keep.tile([P, 1], F32)
        nc.vector.memset(one[:], 1.0)
        warm_sqrt = keep.tile([P, 1], F32)
        nc.scalar.activation(out=warm_sqrt[:], in_=one[:], func=ACT.Sqrt)

        planes = [keep.tile([P, PACK, PLANE], BF16, name="planes%d" % r) for r in range(PLANE_BUFS)]
        cut_planes = [
            [keep.tile([P, PACK, MOVED[b]], BF16, name="cut%d_%d" % (b, r)) for r in range(PLANE_BUFS)]
            for b in range(BATCH)
        ]
        part_planes = [
            [keep.tile([P, PACK, min(hi, PAIRS) - lo], BF16, name="part%d_%d" % (r, lo)) for lo, hi in windows]
            for r, windows in enumerate(LAST_WINDOWS)
        ]
        for r in range(PLANE_BUFS):
            nc.gpsimd.memset(planes[r][:, :, DIAGONAL:PLANE], 0.0)
            nc.gpsimd.memset(cut_planes[1][r][:, :, PAIRS : MOVED[1]], 0.0)
        grouped = [
            [keep.tile([P, COLS, PACK], BF16, align_bytes=64, name="grouped%d_%d" % (b, r)) for r in range(GROUPED_BUFS)]
            for b in range(BATCH)
        ]
        for b in range(BATCH):
            for r in range(GROUPED_BUFS):
                nc.gpsimd.memset(grouped[b][r][:, MOVED[b] : COLS, :], 0.0)

        pair_diff = keep.tile([P, COLS], BF16)
        nc.vector.memset(pair_diff[:, PAIRS:COLS], 0.0)
        for m, first, blocks, offset, stride in SEGMENTS:
            halves = ident_bf[:, 2 * m * first : 2 * m * (first + blocks)].rearrange(
                "i (q two m) -> i q two m", two=2, m=m
            )
            nc.vector.tensor_sub(
                out=pair_diff[:, offset : offset + blocks * m * m].rearrange("i (q a c) -> i q a c", a=m, c=m),
                in0=halves[:, :, 0, :].unsqueeze(3).to_broadcast([P, blocks, m, m]),
                in1=halves[:, :, 1, :].unsqueeze(2).to_broadcast([P, blocks, m, m]),
            )

        diff = psum.tile([P, PART_COLS, BATCH * DIM], F32)
        for l in range(PART_COLS):
            nc.tensor.matmul(
                out=diff[:, l, :],
                lhsT=pair_diff[:, l * P : (l + 1) * P],
                rhs=points[:].rearrange("i b c -> i (b c)"),
                start=True,
                stop=True,
            )
        squares = keep.tile([P, PART_COLS, BATCH * DIM], F32)
        nc.scalar.activation(out=squares[:], in_=diff[:], func=ACT.Square)
        sq_dist = keep.tile([P, PART_COLS, BATCH], F32)
        nc.vector.tensor_reduce(
            out=sq_dist[:], in_=squares[:].rearrange("p l (b c) -> p l b c", c=DIM), axis=AXIS.X, op=ALU.add
        )
        dist_col = keep.tile([P, PART_COLS, BATCH], F32)
        nc.scalar.activation(out=dist_col[:], in_=sq_dist[:], func=ACT.Sqrt)
        warm_silu = keep.tile([P, 1], F32)
        nc.scalar.activation(out=warm_silu[:], in_=one[:], func=ACT.Silu)

        turned = psum.tile([P, PACK + 1, P], BF16)
        for t in range(PACK):
            nc.tensor.transpose(turned[:, t, :], rows[:].rearrange("r (p t) -> r t p", t=PACK)[:, t, :], ident_bf[:])
        affine = keep.tile([P, PACK, 2 * PASSES], F32)
        nc.vector.tensor_copy(out=affine[:], in_=turned[:, 0:PACK, 0 : 2 * PASSES])

        dist = keep.tile([P, USED], F32)
        spread = [psum.tile([P, COLS], F32, name="spread%d" % b) for b in range(BATCH)]
        for b in range(BATCH):
            for l in range(PART_COLS):
                nc.tensor.transpose(
                    spread[b][:, l * P : (l + 1) * P], dist_col[:, l, b : b + 1].to_broadcast([P, P]), ident_f32[:]
                )

        nc.tensor.transpose(turned[:, PACK, :], b2_row[:], ident_bf[:])
        b2_col = keep.tile([P, 1], F32)

        def copy_dist(b):
            cols = PAIRS + b
            nc.vector.tensor_copy(out=dist[:, BASE[b] : BASE[b] + cols], in_=spread[b][:, 0:cols])

        copy_dist(1)

        w2_codes = keep.tile([P, PASSES * HEADS], U32, align_bytes=64)
        w2_scales = keep.tile([P, PASSES * HEADS], U8, align_bytes=64)

        def regroup_w2(first):
            w2_grouped = w2_stage.tile([P, CHUNK * HEADS, PACK], BF16, align_bytes=64)
            for g in range(CHUNK):
                regroup(
                    nc,
                    w2_grouped[:, g * HEADS : (g + 1) * HEADS, :],
                    w2_raw[:, first + g, :].rearrange("p (t k) -> p t k", t=PACK),
                )
            return w2_grouped

        def quantise_w2(first, w2_grouped):
            cols = slice(first * HEADS, (first + CHUNK) * HEADS)
            nc.vector.quantize_mx(
                out=w2_codes[:, cols].bitcast(FP8X4),
                scales=w2_scales[:, cols],
                in_=w2_grouped[:].rearrange("p w t -> p (w t)"),
            )

        quantise_w2(0, regroup_w2(0))

        acc0 = [psum.tile([P, COLS], F32, name="acc0_%d" % lo) for lo, hi, segments in PARTS]
        acc1 = psum.tile([P, COLS], F32)

        def silu(g, dst, src):
            for t in range(PACK):
                nc.scalar.activation(
                    out=dst[:, t, 0 : src.shape[1]],
                    in_=src,
                    func=ACT.Silu,
                    scale=affine[:, t, g : g + 1],
                    bias=affine[:, t, PASSES + g : PASSES + g + 1],
                )

        def regroup_h(g, b, src, lo=0):
            regroup(nc, grouped[b][g % GROUPED_BUFS][:, lo : lo + src.shape[2], :], src)

        def regroup_batch(g, b):
            regroup_h(g, b, cut_planes[b][g % PLANE_BUFS][:])

        def operand():
            codes = h_stage.tile([P, COLS], U32, align_bytes=64)
            scales = h_stage.tile([P, COLS], U8, align_bytes=64)
            return codes, scales

        def quantise(g, b, h, lo=0, hi=COLS):
            codes, scales = h
            nc.vector.quantize_mx(
                out=codes[:, lo:hi].bitcast(FP8X4),
                scales=scales[:, lo:hi],
                in_=grouped[b][g % GROUPED_BUFS][:, lo:hi, :].rearrange("p w t -> p (w t)"),
            )

        def multiply(g, sums, h, lo, hi):
            codes, scales = h
            nc.tensor.matmul_mx(
                out=sums[:, 0 : hi - lo],
                lhsT=w2_codes[:, g * HEADS : (g + 1) * HEADS].bitcast(FP8X4),
                lhsT_scale=w2_scales[:, g * HEADS : (g + 1) * HEADS],
                rhs=codes[:, lo:hi].bitcast(FP8X4),
                rhs_scale=scales[:, lo:hi],
                start=(g == 0),
                stop=(g == PASSES - 1),
            )

        def quantise_and_multiply(g, b):
            h = operand()
            quantise(g, b, h)
            if b == 1:
                multiply(g, acc1, h, 0, COLS)
            else:
                for sums, (lo, hi, segments) in zip(acc0, PARTS):
                    multiply(g, sums, h, lo, hi)

        for b in range(BATCH):
            if b == 0:
                silu(0, cut_planes[b][0], spread[b][:, 0:PAIRS])
                copy_dist(b)
            else:
                silu(0, cut_planes[b][0], dist[:, BASE[b] : USED])
            regroup_batch(0, b)
            quantise_and_multiply(0, b)
        for g in range(1, PASSES - TAIL_PASSES):
            silu(g, planes[g % PLANE_BUFS], dist[:])
            for b in range(BATCH):
                regroup_h(g, b, planes[g % PLANE_BUFS][:, :, BASE[b] : BASE[b] + MOVED[b]])
            for b in range(BATCH):
                quantise_and_multiply(g, b)
            chunk = (g // CHUNK_EVERY + 1) * CHUNK
            if g % CHUNK_EVERY == 1 and chunk < PASSES:
                quantise_w2(chunk, regroup_w2(chunk))

        nc.vector.tensor_copy(out=b2_col[:], in_=turned[:, PACK, 0:1])

        result = keep.tile([P, BATCH, POINTS * OUT_ROW], F32)

        def on_vector(dst, src):
            nc.vector.tensor_scalar_add(out=dst, in0=src, scalar1=b2_col[:, 0:1])

        def on_scalar(dst, src):
            nc.scalar.activation(out=dst, in_=src, func=ACT.Identity, bias=b2_col[:, 0:1])

        def place(b, sums, lo, segments):
            copies = []
            for m, first, blocks, offset, stride in segments:
                pairs = sums[:, offset - lo : offset - lo + blocks * stride].rearrange("k (q s) -> k q s", s=stride)
                pairs = pairs[:, :, 0 : m * m]
                squares_2m = result[:, b, :].rearrange("k (q w) -> k q w", w=2 * m * OUT_ROW)
                squares_2m = squares_2m[:, first : first + blocks, :]
                top = squares_2m[:, :, 0 : m * POINTS].rearrange("k q (a x) -> k q a x", x=POINTS)
                bottom = squares_2m[:, :, m * POINTS : 2 * m * POINTS].rearrange("k q (c x) -> k q c x", x=POINTS)
                copies.append((top[:, :, :, m : 2 * m], pairs.rearrange("k q (a c) -> k q a c", a=m)))
                copies.append((bottom[:, :, :, 0:m], pairs.rearrange("k q (a c) -> k q c a", a=m)))
            return copies

        def place_diagonals():
            return (
                result[:].rearrange("k b (i w) -> k b i w", w=OUT_ROW)[:, :, :, 0],
                acc1[:, PAIRS : PAIRS + 1].unsqueeze(1).to_broadcast([P, BATCH, POINTS]),
            )

        def store(b, first=0, last=POINTS):
            nc.sync.dma_start(
                out=out[b, :, first:last, :].rearrange("k i j -> k (i j)"),
                in_=result[:, b, first * POINTS : last * POINTS],
            )

        jobs = []
        for g in range(PASSES - TAIL_PASSES, PASSES):
            jobs.append((g, 1, cut_planes[1][g % PLANE_BUFS], 0, COLS))
        for g in range(PASSES - TAIL_PASSES, PASSES - 2):
            jobs.append((g, 0, cut_planes[0][g % PLANE_BUFS], 0, COLS))
        for g in (PASSES - 2, PASSES - 1):
            for plane, (lo, hi) in zip(part_planes[g % 2], LAST_WINDOWS[g % 2]):
                jobs.append((g, 0, plane, lo, hi))
        copies = place(1, acc1, 0, JOINED) + [place_diagonals()]
        operands = {}
        waiting = []

        def finish(g, b, lo, hi, pieces):
            if (g, b) not in operands:
                operands[g, b] = operand()
            for first, last in pieces:
                quantise(g, b, operands[g, b], first, last)
            if b == 1:
                multiply(g, acc1, operands[g, b], lo, hi)
            else:
                for sums, (first, last, segments) in zip(acc0, PARTS):
                    if lo <= first and last <= hi:
                        multiply(g, sums, operands[g, b], first, last)

        def halves(lo, hi):
            mid = (lo + hi) // 2
            return [(lo, mid), (mid, hi)] if hi - lo >= 256 else [(lo, hi)]

        for n, (g, b, plane, lo, hi) in enumerate(jobs):
            silu(g, plane, dist[:, BASE[b] + lo : BASE[b] + min(hi, PAIRS + b)])
            pieces = halves(lo, hi) if b == 0 else [(lo, hi)]
            for first, last in pieces:
                regroup_h(g, b, plane[:, :, first - lo : min(last - lo, plane.shape[2])], first)
            for job in waiting:
                finish(*job)
            waiting = [(g, b, lo, hi, pieces)]
            if b == 0:
                if n > TAIL_PASSES:
                    for dst, src in copies[:COPIES_PER_JOB]:
                        on_vector(dst, src)
                    copies = copies[COPIES_PER_JOB:]
                finish(*waiting.pop())
        assert not copies
        store(1)
        for dst, src in place(0, acc0[0], PARTS[0][0], PARTS[0][2]):
            on_scalar(dst, src)
        for dst, src in place(0, acc0[1], PARTS[1][0], PARTS[1][2]):
            on_vector(dst, src)
        store(0, 0, POINTS // 2)
        for dst, src in place(0, acc0[2], PARTS[2][0], PARTS[2][2]):
            on_scalar(dst, src)
        store(0, POINTS // 2, POINTS)
